import numpy as np
import ml_dtypes


def mxq(x, axis, fmt="e4m3"):
    dtype, down = {"e4m3": (ml_dtypes.float8_e4m3fn, 7), "e5m2": (ml_dtypes.float8_e5m2, 14)}[fmt]
    v = np.moveaxis(np.asarray(x, np.float32).astype(ml_dtypes.bfloat16).astype(np.float64), axis, -1)
    blocks = v.reshape(v.shape[:-1] + (-1, 32))
    amax = np.abs(blocks).max(-1, keepdims=True)
    byte = np.maximum(np.where(amax > 0, np.frexp(amax)[1] - 1 + 127, 0) - down, 1)
    scale = np.exp2(byte - 127.0)
    codes = (blocks / scale).astype(np.float32).astype(dtype).astype(np.float64)
    return np.moveaxis((codes * scale).reshape(v.shape), -1, axis)


WIDE = False


def mx_kscale(k):
    if not WIDE:
        return np.ones(k)
    levels = np.array([30, -30])
    if k % 512:
        return np.exp2(np.random.permutation(np.resize(levels, k // 32))).repeat(32)
    a = np.empty((k // 512, 16))
    for p in range(k // 512):
        a[p, :8] = np.random.permutation(np.resize(levels, 8))
        for g in range(8):
            far = levels[np.abs(levels - a[p, g]) >= 10]
            a[p, g + 8] = far[np.random.randint(len(far))]
    return np.exp2(a.ravel()).repeat(32)


BF16 = ml_dtypes.bfloat16


def bf(x):
    return np.asarray(x, np.float32).astype(BF16)


def f64(x):
    return np.asarray(x).astype(np.float64)


B, T, D, NH, HD, QB = 1, 1024, 1024, 8, 256, 512
E = NH * HD
HD2 = HD // 2
EPS = 2.0 ** -23
ROPE_BASE = 10000.0


def rms_norm(u):
    ms = np.mean(np.square(u), axis=-1, keepdims=True)
    return u * (1.0 / np.sqrt(ms + EPS))


def rotary_cos_sin():
    inv_freq = 1.0 / (ROPE_BASE ** (np.arange(0, HD, 2) / HD))
    freqs = np.outer(np.arange(T), inv_freq)
    return np.cos(freqs)[None, :, None, :], np.sin(freqs)[None, :, None, :]


def apply_rotary_emb(u, cos, sin):
    u1, u2 = u[..., :HD2], u[..., HD2:]
    return np.concatenate([u1 * cos + u2 * sin, -u1 * sin + u2 * cos], axis=-1)


def setup_inputs():
    s = mx_kscale(D)
    return {"x": bf(np.random.standard_normal((B, T, D)) * s),
            "Wq": bf(np.random.standard_normal((E, D)) / np.sqrt(D) / s[None, :]),
            "Wk": bf(np.random.standard_normal((E, D)) / np.sqrt(D) / s[None, :])}


def reference(x, Wq, Wk):
    xq = mxq(f64(x), 2, "e5m2")
    q = (xq @ mxq(f64(Wq), 1, "e5m2").T).reshape(B, T, NH, HD)
    k = (xq @ mxq(f64(Wk), 1, "e5m2").T).reshape(B, T, NH, HD)
    cos, sin = rotary_cos_sin()
    return apply_rotary_emb(rms_norm(q), cos, sin), apply_rotary_emb(rms_norm(k), cos, sin)

@@ -1,0 +1,265 @@
+import math
+from contextlib import ExitStack
+
+import concourse.mybir as mybir
+from concourse.masks import make_identity
+
+T, D, NH, HD = 1024, 1024, 8, 256
+E = NH * HD
+HALF = HD // 2
+EPS = 2.0 ** -23
+ROPE_BASE = 10000.0
+FLOPS = 2 * T * D * 2 * E
+
+F32 = mybir.dt.float32
+BF16 = mybir.dt.bfloat16
+I32 = mybir.dt.int32
+U32 = mybir.dt.uint32
+U8 = mybir.dt.uint8
+E5M2X4 = mybir.dt.float8_e5m2_x4
+ALU = mybir.AluOpType
+ACT = mybir.ActivationFunctionType
+
+P = 128
+K_PASS = 512
+PASSES = D // K_PASS
+PASS_WORDS = K_PASS // 2
+BANK = 512
+HEADS_PER_BANK = BANK // HD
+ROW_TILES = BANK // P
+TOKEN_TILES = T // P
+CHUNKS = 2 * E // BANK
+STEPS = CHUNKS * TOKEN_TILES
+
+
+def tile_mixerdiffattention_pa_kernel(tc, x, Wq, Wk, out_0, out_1):
+    nc = tc.nc
+    x_rows = x.rearrange("b t d -> (b t) d")
+    outs = [o.rearrange("b t h d -> (b t) (h d)") for o in (out_0, out_1)]
+    chunks_per_weight = E // BANK
+
+    def chunk_rows(c):
+        weight = (Wq, Wk)[c // chunks_per_weight]
+        first = (c % chunks_per_weight) * BANK
+        return weight[first : first + BANK, :]
+
+    with ExitStack() as ctx:
+        keep = ctx.enter_context(tc.tile_pool(name="keep", bufs=1))
+        w_raw_pool = ctx.enter_context(tc.tile_pool(name="w_raw", bufs=3 * ROW_TILES))
+        w_pool = ctx.enter_context(tc.tile_pool(name="w_mx", bufs=2))
+        work = ctx.enter_context(tc.tile_pool(name="work", bufs=4))
+        result_pool = ctx.enter_context(tc.tile_pool(name="result", bufs=10))
+        small = ctx.enter_context(tc.tile_pool(name="small", bufs=8))
+        turn_psum = ctx.enter_context(tc.psum_pool(name="turn_psum", bufs=3))
+        acc_psum = ctx.enter_context(tc.psum_pool(name="acc_psum", bufs=5))
+        ctx.enter_context(tc.manual_schedule())
+
+        x_raw = [keep.tile([P, D], BF16, name="x_raw%d" % i) for i in range(TOKEN_TILES)]
+        x_grouped = keep.tile([P, TOKEN_TILES, PASSES * P * 4], BF16, align_bytes=64)
+        x_codes = keep.tile([P, TOKEN_TILES, PASSES * P], U32, align_bytes=64)
+        x_scales = keep.tile([P, TOKEN_TILES, PASSES * P], U8, align_bytes=64)
+        w_raw, w_grouped, w_codes, w_scales = {}, {}, {}, {}
+        turned, acc, mean_sq, inv_rms, by_cos, by_sin, result = {}, {}, {}, {}, {}, {}, {}
+
+        def load_x(i):
+            nc.sync.dma_start(out=x_raw[i][:], in_=x_rows[i * P : (i + 1) * P, :])
+
+        def load_w(c):
+            for s in range(ROW_TILES):
+                rows = w_raw_pool.tile([P, D], BF16, name="w_rows")
+                nc.sync.dma_start(out=rows[:], in_=chunk_rows(c)[s * P : (s + 1) * P, :])
+                w_raw[c, s] = rows
+
+        def turn(key, rows):
+            words = rows[:].bitcast(F32)
+            bank = turn_psum.tile([P, PASSES, 2, P], F32, name="turned")
+            for g in range(PASSES):
+                for u in range(2):
+                    nc.tensor.transpose(bank[:, g, u, :], words[:, g * PASS_WORDS + u : (g + 1) * PASS_WORDS : 2], identity[:])
+            turned[key] = bank
+
+        def copy_on(engine, out, in_):
+            if engine == "vector":
+                nc.vector.tensor_copy(out=out, in_=in_)
+            else:
+                nc.scalar.copy(out=out, in_=in_)
+
+        def group_x(i, engine):
+            target = x_grouped[:, i, :].bitcast(F32).rearrange("p (g r u) -> p g r u", g=PASSES, u=2)
+            copy_on(engine, target, turned["x", i][:].rearrange("p g u r -> p g r u"))
+
+        def group_w(c, s, engine):
+            if s == 0:
+                w_grouped[c] = w_pool.tile([P, PASSES * BANK * 4], BF16, name="w_grouped", align_bytes=64)
+            words = w_grouped[c][:].bitcast(F32).rearrange("p (g n u) -> p g n u", g=PASSES, u=2)
+            copy_on(engine, words[:, :, s * P : (s + 1) * P, :], turned[c, s][:].rearrange("p g u r -> p g r u"))
+
+        def quantize_x(first, count):
+            tiles = slice(first, first + count)
+            nc.vector.quantize_mx(
+                out=x_codes[:, tiles, :].rearrange("p i c -> p (i c)").bitcast(E5M2X4),
+                scales=x_scales[:, tiles, :].rearrange("p i c -> p (i c)"),
+                in_=x_grouped[:, tiles, :].rearrange("p i c -> p (i c)"),
+            )
+
+        def quantize_w(c):
+            w_codes[c] = w_pool.tile([P, PASSES * BANK], U32, name="w_codes", align_bytes=64)
+            w_scales[c] = w_pool.tile([P, PASSES * BANK], U8, name="w_scales", align_bytes=64)
+            nc.vector.quantize_mx(out=w_codes[c][:].bitcast(E5M2X4), scales=w_scales[c][:], in_=w_grouped[c][:])
+
+        def project(n):
+            c, i = divmod(n, TOKEN_TILES)
+            acc[n] = acc_psum.tile([P, BANK], F32, name="acc")
+            for g in range(PASSES):
+                tokens = slice(g * P, (g + 1) * P)
+                features = slice(g * BANK, (g + 1) * BANK)
+                nc.tensor.matmul_mx(
+                    out=acc[n][:],
+                    lhsT=x_codes[:, i, tokens].bitcast(E5M2X4),
+                    lhsT_scale=x_scales[:, i, tokens],
+                    rhs=w_codes[c][:, features].bitcast(E5M2X4),
+                    rhs_scale=w_scales[c][:, features],
+                    start=(g == 0),
+                    stop=(g == PASSES - 1),
+                )
+
+        def mean_square(n, h):
+            if h == 0:
+                mean_sq[n] = small.tile([P, HEADS_PER_BANK], F32, name="mean_sq")
+            squares = work.tile([P, HD], BF16, name="squares")
+            nc.scalar.activation(
+                out=squares[:], in_=acc[n][:, h * HD : (h + 1) * HD], func=ACT.Square,
+                scale=1.0 / math.sqrt(HD), accum_out=mean_sq[n][:, h : h + 1],
+            )
+
+        def inverse_rms(n):
+            inv_rms[n] = small.tile([P, HEADS_PER_BANK], F32, name="inv_rms")
+            nc.scalar.activation(out=inv_rms[n][:], in_=mean_sq[n][:], func=ACT.Abs_reciprocal_sqrt, bias=eps[:])
+
+        def products(n):
+            i = n % TOKEN_TILES
+            by_cos[n] = work.tile([P, HEADS_PER_BANK, 2, HALF], F32, name="by_cos")
+            by_sin[n] = work.tile([P, HEADS_PER_BANK, 2, HALF], F32, name="by_sin")
+            u = acc[n][:].rearrange("p (h a j) -> p h a j", h=HEADS_PER_BANK, a=2)
+            cos_twice = cos_table[:, i, :].unsqueeze(1).to_broadcast([P, 2, HALF])
+            for h in range(HEADS_PER_BANK):
+                factor = inv_rms[n][:, h : h + 1]
+                nc.vector.scalar_tensor_tensor(
+                    out=by_cos[n][:, h, :, :], in0=u[:, h, :, :], scalar=factor, in1=cos_twice,
+                    op0=ALU.mult, op1=ALU.mult,
+                )
+                nc.vector.scalar_tensor_tensor(
+                    out=by_sin[n][:, h, :, :], in0=u[:, h, ::-1, :], scalar=factor, in1=sin_table[:, i, :, :],
+                    op0=ALU.mult, op1=ALU.mult,
+                )
+
+        def finish(n):
+            c, i = divmod(n, TOKEN_TILES)
+            result[n] = result_pool.tile([P, BANK], F32, name="result")
+            nc.gpsimd.tensor_tensor(
+                out=result[n][:],
+                in0=by_cos[n][:].rearrange("p h a j -> p (h a j)"),
+                in1=by_sin[n][:].rearrange("p h a j -> p (h a j)"),
+                op=ALU.add,
+            )
+            first = (c % chunks_per_weight) * BANK
+            nc.sync.dma_start(
+                out=outs[c // chunks_per_weight][i * P : (i + 1) * P, first : first + BANK], in_=result[n][:]
+            )
+
+        load_x(0)
+        load_w(0)
+        for i in range(1, TOKEN_TILES):
+            load_x(i)
+        load_w(1)
+        load_w(2)
+
+        identity = keep.tile([P, P], F32)
+        make_identity(nc, identity[:])
+        position = keep.tile([P, TOKEN_TILES], F32)
+        nc.gpsimd.iota(position[:], pattern=[[P, TOKEN_TILES]], base=0, channel_multiplier=1,
+                       allow_small_or_imprecise_dtypes=True)
+
+        ones = keep.tile([P, 1], F32)
+        nc.vector.memset(ones[:], 1.0)
+        eps = keep.tile([P, 1], F32)
+        nc.vector.memset(eps[:], EPS)
+        quarter_turn = keep.tile([P, 1], F32)
+        nc.vector.tensor_scalar(out=quarter_turn[:], in0=ones[:], scalar1=math.pi / 2, scalar2=None, op0=ALU.mult)
+        ratio = ROPE_BASE ** (-1.0 / HALF)
+        rate = keep.tile([P, HALF], F32)
+        known = 4
+        for j in range(known):
+            nc.vector.tensor_scalar(out=rate[:, j : j + 1], in0=ones[:], scalar1=ratio ** j / (2 * math.pi),
+                                    scalar2=None, op0=ALU.mult)
+        for radix in (4, 8):
+            for m in range(1, radix):
+                nc.vector.tensor_scalar(out=rate[:, m * known : (m + 1) * known], in0=rate[:, 0:known],
+                                        scalar1=ratio ** (m * known), scalar2=None, op0=ALU.mult)
+            known = known * radix
+
+        whole_turns = keep.tile([P, TOKEN_TILES, HALF], I32)
+        part_turn = keep.tile([P, TOKEN_TILES, HALF], F32)
+        part_size = keep.tile([P, TOKEN_TILES, HALF], F32)
+        cos_table = keep.tile([P, TOKEN_TILES, HALF], F32)
+        sin_table = keep.tile([P, TOKEN_TILES, 2, HALF], F32)
+        for i in range(TOKEN_TILES):
+            nc.vector.tensor_scalar(out=whole_turns[:, i, :], in0=rate[:], scalar1=position[:, i : i + 1],
+                                    scalar2=None, op0=ALU.mult)
+        for i in range(TOKEN_TILES):
+            nc.vector.scalar_tensor_tensor(out=part_turn[:, i, :], in0=rate[:], scalar=position[:, i : i + 1],
+                                           in1=whole_turns[:, i, :], op0=ALU.mult, op1=ALU.subtract)
+        for half in range(2):
+            tiles = slice(half * TOKEN_TILES // 2, (half + 1) * TOKEN_TILES // 2)
+            nc.scalar.activation(out=sin_table[:, tiles, 0, :], in_=part_turn[:, tiles, :], func=ACT.Sin, scale=2 * math.pi)
+            nc.scalar.activation(out=part_size[:, tiles, :], in_=part_turn[:, tiles, :], func=ACT.Abs)
+            nc.gpsimd.tensor_scalar(out=sin_table[:, tiles, 1, :], in0=sin_table[:, tiles, 0, :], scalar1=-1.0,
+                                    scalar2=0.0, op0=ALU.mult, op1=ALU.add)
+        nc.scalar.activation(out=cos_table[:], in_=part_size[:], func=ACT.Sin, scale=-2 * math.pi, bias=quarter_turn[:])
+
+        turn(("x", 0), x_raw[0])
+        group_x(0, "vector")
+        for s in range(ROW_TILES):
+            turn((0, s), w_raw[0, s])
+            group_w(0, s, "vector")
+            if s == 0:
+                quantize_x(0, 1)
+        turn(("x", 1), x_raw[1])
+        group_x(1, "vector")
+        quantize_w(0)
+        quantize_x(1, 1)
+        project(0)
+        for i in (2, 3):
+            turn(("x", i), x_raw[i])
+            group_x(i, "vector")
+
+        for n in range(STEPS + 1):
+            c, i = divmod(n, TOKEN_TILES)
+            first_turn = 3 if c == 0 else 1
+            if 0 < n < STEPS:
+                project(n)
+            if n < STEPS:
+                mean_square(n, 0)
+            if n > 0:
+                inverse_rms(n - 1)
+            if n < STEPS:
+                mean_square(n, 1)
+            if c == 0 and i < 4:
+                turn(("x", i + 4), x_raw[i + 4])
+                group_x(i + 4, "scalar")
+            if c + 1 < CHUNKS:
+                s = i - first_turn
+                if s in (0, 2):
+                    turn((c + 1, s), w_raw[c + 1, s])
+                    turn((c + 1, s + 1), w_raw[c + 1, s + 1])
+                if 0 <= s < ROW_TILES:
+                    group_w(c + 1, s, "scalar")
+                if s == ROW_TILES:
+                    quantize_w(c + 1)
+            if c == 0 and i in (0, 2, 4):
+                quantize_x(i + 2, 2)
+            if n > 0:
+                products(n - 1)
+                finish(n - 1)
+            if i == TOKEN_TILES - 1 and c + 3 < CHUNKS:
+                load_w(c + 3)

@@ -30,6 +30,7 @@ ROW_TILES = BANK // P
 TOKEN_TILES = T // P
 CHUNKS = 2 * E // BANK
 STEPS = CHUNKS * TOKEN_TILES
+GROUP = 4
 
 
 def tile_mixerdiffattention_pa_kernel(tc, x, Wq, Wk, out_0, out_1):
@@ -45,10 +46,10 @@ def tile_mixerdiffattention_pa_kernel(tc, x, Wq, Wk, out_0, out_1):
 
     with ExitStack() as ctx:
         keep = ctx.enter_context(tc.tile_pool(name="keep", bufs=1))
-        w_raw_pool = ctx.enter_context(tc.tile_pool(name="w_raw", bufs=3 * ROW_TILES))
+        w_raw_pool = ctx.enter_context(tc.tile_pool(name="w_raw", bufs=3))
         w_pool = ctx.enter_context(tc.tile_pool(name="w_mx", bufs=2))
-        work = ctx.enter_context(tc.tile_pool(name="work", bufs=4))
-        result_pool = ctx.enter_context(tc.tile_pool(name="result", bufs=10))
+        work = ctx.enter_context(tc.tile_pool(name="work", bufs=3))
+        result_pool = ctx.enter_context(tc.tile_pool(name="result", bufs=4))
         small = ctx.enter_context(tc.tile_pool(name="small", bufs=8))
         turn_psum = ctx.enter_context(tc.psum_pool(name="turn_psum", bufs=3))
         acc_psum = ctx.enter_context(tc.psum_pool(name="acc_psum", bufs=5))
@@ -59,19 +60,20 @@ def tile_mixerdiffattention_pa_kernel(tc, x, Wq, Wk, out_0, out_1):
         x_codes = keep.tile([P, TOKEN_TILES, PASSES * P], U32, align_bytes=64)
         x_scales = keep.tile([P, TOKEN_TILES, PASSES * P], U8, align_bytes=64)
         w_raw, w_grouped, w_codes, w_scales = {}, {}, {}, {}
-        turned, acc, mean_sq, inv_rms, by_cos, by_sin, result = {}, {}, {}, {}, {}, {}, {}
+        turned, acc, mean_sq, inv_rms, by_cos, by_sin = {}, {}, {}, {}, {}, {}
 
         def load_x(i):
             nc.sync.dma_start(out=x_raw[i][:], in_=x_rows[i * P : (i + 1) * P, :])
 
         def load_w(c):
-            for s in range(ROW_TILES):
-                rows = w_raw_pool.tile([P, D], BF16, name="w_rows")
-                nc.sync.dma_start(out=rows[:], in_=chunk_rows(c)[s * P : (s + 1) * P, :])
-                w_raw[c, s] = rows
+            w_raw[c] = w_raw_pool.tile([P, ROW_TILES, D], BF16, name="w_rows")
+            rows = chunk_rows(c).rearrange("(s m) k -> m s k", s=ROW_TILES)
+            piece = 1 if c == 0 else ROW_TILES
+            for s in range(0, ROW_TILES, piece):
+                nc.sync.dma_start(out=w_raw[c][:, s : s + piece, :], in_=rows[:, s : s + piece, :])
 
         def turn(key, rows):
-            words = rows[:].bitcast(F32)
+            words = rows.bitcast(F32)
             bank = turn_psum.tile([P, PASSES, 2, P], F32, name="turned")
             for g in range(PASSES):
                 for u in range(2):
@@ -138,34 +140,47 @@ def tile_mixerdiffattention_pa_kernel(tc, x, Wq, Wk, out_0, out_1):
 
         def products(n):
             i = n % TOKEN_TILES
-            by_cos[n] = work.tile([P, HEADS_PER_BANK, 2, HALF], F32, name="by_cos")
-            by_sin[n] = work.tile([P, HEADS_PER_BANK, 2, HALF], F32, name="by_sin")
+            first, size = group_of[n]
+            if n == first:
+                by_cos[first] = work.tile([P, GROUP, HEADS_PER_BANK, 2, HALF], F32, name="by_cos")
+                by_sin[first] = work.tile([P, GROUP, HEADS_PER_BANK, 2, HALF], F32, name="by_sin")
             u = acc[n][:].rearrange("p (h a j) -> p h a j", h=HEADS_PER_BANK, a=2)
             cos_twice = cos_table[:, i, :].unsqueeze(1).to_broadcast([P, 2, HALF])
             for h in range(HEADS_PER_BANK):
                 factor = inv_rms[n][:, h : h + 1]
                 nc.vector.scalar_tensor_tensor(
-                    out=by_cos[n][:, h, :, :], in0=u[:, h, :, :], scalar=factor, in1=cos_twice,
+                    out=by_cos[first][:, n - first, h, :, :], in0=u[:, h, :, :], scalar=factor, in1=cos_twice,
                     op0=ALU.mult, op1=ALU.mult,
                 )
                 nc.vector.scalar_tensor_tensor(
-                    out=by_sin[n][:, h, :, :], in0=u[:, h, ::-1, :], scalar=factor, in1=sin_table[:, i, :, :],
+                    out=by_sin[first][:, n - first, h, :, :], in0=u[:, h, ::-1, :], scalar=factor, in1=sin_table[:, i, :, :],
                     op0=ALU.mult, op1=ALU.mult,
                 )
 
-        def finish(n):
-            c, i = divmod(n, TOKEN_TILES)
-            result[n] = result_pool.tile([P, BANK], F32, name="result")
-            nc.gpsimd.tensor_tensor(
-                out=result[n][:],
-                in0=by_cos[n][:].rearrange("p h a j -> p (h a j)"),
-                in1=by_sin[n][:].rearrange("p h a j -> p (h a j)"),
+        def finish(engine, first, lo, hi):
+            c, i = divmod(first, TOKEN_TILES)
+            result = result_pool.tile([P, GROUP * BANK], F32, name="result")
+            width = (hi - lo) * BANK
+            engine.tensor_tensor(
+                out=result[:, 0:width],
+                in0=by_cos[first][:, lo:hi].rearrange("p i h a j -> p (i h a j)"),
+                in1=by_sin[first][:, lo:hi].rearrange("p i h a j -> p (i h a j)"),
                 op=ALU.add,
             )
-            first = (c % chunks_per_weight) * BANK
+            column = (c % chunks_per_weight) * BANK
+            target = outs[c // chunks_per_weight][(i + lo) * P : (i + hi) * P, column : column + BANK]
             nc.sync.dma_start(
-                out=outs[c // chunks_per_weight][i * P : (i + 1) * P, first : first + BANK], in_=result[n][:]
+                out=target.rearrange("(i p) n -> p i n", p=P),
+                in_=result[:, 0:width].rearrange("p (i n) -> p i n", n=BANK),
             )
+
+        sizes = [1, 1, 2, 2, 2] + [GROUP] * (2 * CHUNKS - 3) + [2, 2]
+        group_of = {}
+        first = 0
+        for size in sizes:
+            for n in range(first, first + size):
+                group_of[n] = (first, size)
+            first += size
 
         load_x(0)
         load_w(0)
@@ -217,25 +232,25 @@ def tile_mixerdiffattention_pa_kernel(tc, x, Wq, Wk, out_0, out_1):
                                     scalar2=0.0, op0=ALU.mult, op1=ALU.add)
         nc.scalar.activation(out=cos_table[:], in_=part_size[:], func=ACT.Sin, scale=-2 * math.pi, bias=quarter_turn[:])
 
-        turn(("x", 0), x_raw[0])
+        turn(("x", 0), x_raw[0][:])
         group_x(0, "vector")
         for s in range(ROW_TILES):
-            turn((0, s), w_raw[0, s])
+            turn((0, s), w_raw[0][:, s, :])
             group_w(0, s, "vector")
             if s == 0:
                 quantize_x(0, 1)
-        turn(("x", 1), x_raw[1])
+        turn(("x", 1), x_raw[1][:])
         group_x(1, "vector")
         quantize_w(0)
         quantize_x(1, 1)
         project(0)
         for i in (2, 3):
-            turn(("x", i), x_raw[i])
+            turn(("x", i), x_raw[i][:])
             group_x(i, "vector")
 
         for n in range(STEPS + 1):
             c, i = divmod(n, TOKEN_TILES)
-            first_turn = 3 if c == 0 else 1
+            first_turn = 2 if c == 0 else 0
             if 0 < n < STEPS:
                 project(n)
             if n < STEPS:
@@ -245,21 +260,27 @@ def tile_mixerdiffattention_pa_kernel(tc, x, Wq, Wk, out_0, out_1):
             if n < STEPS:
                 mean_square(n, 1)
             if c == 0 and i < 4:
-                turn(("x", i + 4), x_raw[i + 4])
+                turn(("x", i + 4), x_raw[i + 4][:])
                 group_x(i + 4, "scalar")
             if c + 1 < CHUNKS:
                 s = i - first_turn
                 if s in (0, 2):
-                    turn((c + 1, s), w_raw[c + 1, s])
-                    turn((c + 1, s + 1), w_raw[c + 1, s + 1])
+                    turn((c + 1, s), w_raw[c + 1][:, s, :])
+                    turn((c + 1, s + 1), w_raw[c + 1][:, s + 1, :])
                 if 0 <= s < ROW_TILES:
                     group_w(c + 1, s, "scalar")
-                if s == ROW_TILES:
-                    quantize_w(c + 1)
+            if n > 0:
+                products(n - 1)
+            if c + 1 < CHUNKS and i - first_turn == ROW_TILES:
+                quantize_w(c + 1)
             if c == 0 and i in (0, 2, 4):
                 quantize_x(i + 2, 2)
             if n > 0:
-                products(n - 1)
-                finish(n - 1)
+                first, size = group_of[n - 1]
+                if n == STEPS:
+                    for lo in range(size):
+                        finish(nc.vector, first, lo, lo + 1)
+                elif n == first + size:
+                    finish(nc.gpsimd, first, 0, size)
             if i == TOKEN_TILES - 1 and c + 3 < CHUNKS:
                 load_w(c + 3)

@@ -51,8 +51,8 @@ def tile_mixerdiffattention_pa_kernel(tc, x, Wq, Wk, out_0, out_1):
         work = ctx.enter_context(tc.tile_pool(name="work", bufs=3))
         result_pool = ctx.enter_context(tc.tile_pool(name="result", bufs=4))
         small = ctx.enter_context(tc.tile_pool(name="small", bufs=8))
-        turn_psum = ctx.enter_context(tc.psum_pool(name="turn_psum", bufs=3))
-        acc_psum = ctx.enter_context(tc.psum_pool(name="acc_psum", bufs=5))
+        turn_psum = ctx.enter_context(tc.psum_pool(name="turn_psum", bufs=2))
+        acc_psum = ctx.enter_context(tc.psum_pool(name="acc_psum", bufs=6))
         ctx.enter_context(tc.manual_schedule())
 
         x_raw = [keep.tile([P, D], BF16, name="x_raw%d" % i) for i in range(TOKEN_TILES)]
@@ -60,7 +60,7 @@ def tile_mixerdiffattention_pa_kernel(tc, x, Wq, Wk, out_0, out_1):
         x_codes = keep.tile([P, TOKEN_TILES, PASSES * P], U32, align_bytes=64)
         x_scales = keep.tile([P, TOKEN_TILES, PASSES * P], U8, align_bytes=64)
         w_raw, w_grouped, w_codes, w_scales = {}, {}, {}, {}
-        turned, acc, mean_sq, inv_rms, by_cos, by_sin = {}, {}, {}, {}, {}, {}
+        turned, acc, mean_sq, inv_rms, terms = {}, {}, {}, {}, {}
 
         def load_x(i):
             nc.sync.dma_start(out=x_raw[i][:], in_=x_rows[i * P : (i + 1) * P, :])
@@ -72,9 +72,12 @@ def tile_mixerdiffattention_pa_kernel(tc, x, Wq, Wk, out_0, out_1):
             for s in range(0, ROW_TILES, piece):
                 nc.sync.dma_start(out=w_raw[c][:, s : s + piece, :], in_=rows[:, s : s + piece, :])
 
-        def turn(key, rows):
+        def turn(key, rows, before_projections=False):
             words = rows.bitcast(F32)
-            bank = turn_psum.tile([P, PASSES, 2, P], F32, name="turned")
+            if before_projections:
+                bank = acc_psum.tile([P, PASSES, 2, P], F32, name="acc")
+            else:
+                bank = turn_psum.tile([P, PASSES, 2, P], F32, name="turned")
             for g in range(PASSES):
                 for u in range(2):
                     nc.tensor.transpose(bank[:, g, u, :], words[:, g * PASS_WORDS + u : (g + 1) * PASS_WORDS : 2], identity[:])
@@ -104,19 +107,26 @@ def tile_mixerdiffattention_pa_kernel(tc, x, Wq, Wk, out_0, out_1):
                 in_=x_grouped[:, tiles, :].rearrange("p i c -> p (i c)"),
             )
 
-        def quantize_w(c):
+        def new_w_operand(c):
             w_codes[c] = w_pool.tile([P, PASSES * BANK], U32, name="w_codes", align_bytes=64)
             w_scales[c] = w_pool.tile([P, PASSES * BANK], U8, name="w_scales", align_bytes=64)
-            nc.vector.quantize_mx(out=w_codes[c][:].bitcast(E5M2X4), scales=w_scales[c][:], in_=w_grouped[c][:])
 
-        def project(n):
+        def quantize_w(c, first, width):
+            nc.vector.quantize_mx(
+                out=w_codes[c][:, first : first + width].bitcast(E5M2X4),
+                scales=w_scales[c][:, first : first + width],
+                in_=w_grouped[c][:, 4 * first : 4 * (first + width)],
+            )
+
+        def project(n, heads):
             c, i = divmod(n, TOKEN_TILES)
-            acc[n] = acc_psum.tile([P, BANK], F32, name="acc")
+            width = len(heads) * HD
+            bank = acc_psum.tile([P, BANK], F32, name="acc")
             for g in range(PASSES):
                 tokens = slice(g * P, (g + 1) * P)
-                features = slice(g * BANK, (g + 1) * BANK)
+                features = slice(g * BANK + heads[0] * HD, g * BANK + heads[0] * HD + width)
                 nc.tensor.matmul_mx(
-                    out=acc[n][:],
+                    out=bank[:, 0:width],
                     lhsT=x_codes[:, i, tokens].bitcast(E5M2X4),
                     lhsT_scale=x_scales[:, i, tokens],
                     rhs=w_codes[c][:, features].bitcast(E5M2X4),
@@ -124,36 +134,36 @@ def tile_mixerdiffattention_pa_kernel(tc, x, Wq, Wk, out_0, out_1):
                     start=(g == 0),
                     stop=(g == PASSES - 1),
                 )
+            for place, h in enumerate(heads):
+                acc[n, h] = bank[:, place * HD : (place + 1) * HD]
 
         def mean_square(n, h):
             if h == 0:
                 mean_sq[n] = small.tile([P, HEADS_PER_BANK], F32, name="mean_sq")
-            squares = work.tile([P, HD], BF16, name="squares")
+            squares = small.tile([P, HD], BF16, name="squares")
             nc.scalar.activation(
-                out=squares[:], in_=acc[n][:, h * HD : (h + 1) * HD], func=ACT.Square,
+                out=squares[:], in_=acc[n, h], func=ACT.Square,
                 scale=1.0 / math.sqrt(HD), accum_out=mean_sq[n][:, h : h + 1],
             )
 
-        def inverse_rms(n):
-            inv_rms[n] = small.tile([P, HEADS_PER_BANK], F32, name="inv_rms")
-            nc.scalar.activation(out=inv_rms[n][:], in_=mean_sq[n][:], func=ACT.Abs_reciprocal_sqrt, bias=eps[:])
+        def inverse_rms(n, heads):
+            factors = small.tile([P, len(heads)], F32, name="inv_rms")
+            nc.scalar.activation(out=factors[:], in_=mean_sq[n][:, heads[0] : heads[-1] + 1],
+                                 func=ACT.Abs_reciprocal_sqrt, bias=eps[:])
+            for place, h in enumerate(heads):
+                inv_rms[n, h] = factors[:, place : place + 1]
 
-        def products(n):
+        def products(n, heads):
             i = n % TOKEN_TILES
             first, size = group_of[n]
-            if n == first:
-                by_cos[first] = work.tile([P, GROUP, HEADS_PER_BANK, 2, HALF], F32, name="by_cos")
-                by_sin[first] = work.tile([P, GROUP, HEADS_PER_BANK, 2, HALF], F32, name="by_sin")
-            u = acc[n][:].rearrange("p (h a j) -> p h a j", h=HEADS_PER_BANK, a=2)
-            cos_twice = cos_table[:, i, :].unsqueeze(1).to_broadcast([P, 2, HALF])
-            for h in range(HEADS_PER_BANK):
-                factor = inv_rms[n][:, h : h + 1]
+            if first not in terms:
+                terms[first] = work.tile([P, GROUP * HEADS_PER_BANK, 2, HD], F32, name="terms")
+            for h in heads:
                 nc.vector.scalar_tensor_tensor(
-                    out=by_cos[first][:, n - first, h, :, :], in0=u[:, h, :, :], scalar=factor, in1=cos_twice,
-                    op0=ALU.mult, op1=ALU.mult,
-                )
-                nc.vector.scalar_tensor_tensor(
-                    out=by_sin[first][:, n - first, h, :, :], in0=u[:, h, ::-1, :], scalar=factor, in1=sin_table[:, i, :, :],
+                    out=terms[first][:, (n - first) * HEADS_PER_BANK + h, :, :],
+                    in0=acc[n, h].unsqueeze(1).to_broadcast([P, 2, HD]),
+                    scalar=inv_rms[n, h],
+                    in1=table[:, i, :, :, :].rearrange("p f a j -> p f (a j)"),
                     op0=ALU.mult, op1=ALU.mult,
                 )
 
@@ -161,12 +171,11 @@ def tile_mixerdiffattention_pa_kernel(tc, x, Wq, Wk, out_0, out_1):
             c, i = divmod(first, TOKEN_TILES)
             result = result_pool.tile([P, GROUP * BANK], F32, name="result")
             width = (hi - lo) * BANK
-            engine.tensor_tensor(
-                out=result[:, 0:width],
-                in0=by_cos[first][:, lo:hi].rearrange("p i h a j -> p (i h a j)"),
-                in1=by_sin[first][:, lo:hi].rearrange("p i h a j -> p (i h a j)"),
-                op=ALU.add,
-            )
+            halves = result[:, 0:width].rearrange("p (v a j) -> p v a j", a=2, j=HALF)
+            vectors = slice(lo * HEADS_PER_BANK, hi * HEADS_PER_BANK)
+            by_cos, by_sin = terms[first][:, vectors, 0, :], terms[first][:, vectors, 1, :]
+            engine.tensor_tensor(out=halves[:, :, 0, :], in0=by_cos[:, :, 0:HALF], in1=by_sin[:, :, HALF:HD], op=ALU.add)
+            engine.tensor_tensor(out=halves[:, :, 1, :], in0=by_cos[:, :, HALF:HD], in1=by_sin[:, :, 0:HALF], op=ALU.subtract)
             column = (c % chunks_per_weight) * BANK
             target = outs[c // chunks_per_weight][(i + lo) * P : (i + hi) * P, column : column + BANK]
             nc.sync.dma_start(
@@ -174,7 +183,7 @@ def tile_mixerdiffattention_pa_kernel(tc, x, Wq, Wk, out_0, out_1):
                 in_=result[:, 0:width].rearrange("p (i n) -> p i n", n=BANK),
             )
 
-        sizes = [1, 1, 2, 2, 2] + [GROUP] * (2 * CHUNKS - 3) + [2, 2]
+        sizes = [1, 1, 2, 2, 2] + [GROUP] * (2 * CHUNKS - 4) + [2, 2, GROUP]
         group_of = {}
         first = 0
         for size in sizes:
@@ -216,8 +225,7 @@ def tile_mixerdiffattention_pa_kernel(tc, x, Wq, Wk, out_0, out_1):
         whole_turns = keep.tile([P, TOKEN_TILES, HALF], I32)
         part_turn = keep.tile([P, TOKEN_TILES, HALF], F32)
         part_size = keep.tile([P, TOKEN_TILES, HALF], F32)
-        cos_table = keep.tile([P, TOKEN_TILES, HALF], F32)
-        sin_table = keep.tile([P, TOKEN_TILES, 2, HALF], F32)
+        table = keep.tile([P, TOKEN_TILES, 2, 2, HALF], F32)
         for i in range(TOKEN_TILES):
             nc.vector.tensor_scalar(out=whole_turns[:, i, :], in0=rate[:], scalar1=position[:, i : i + 1],
                                     scalar2=None, op0=ALU.mult)
@@ -226,61 +234,76 @@ def tile_mixerdiffattention_pa_kernel(tc, x, Wq, Wk, out_0, out_1):
                                            in1=whole_turns[:, i, :], op0=ALU.mult, op1=ALU.subtract)
         for half in range(2):
             tiles = slice(half * TOKEN_TILES // 2, (half + 1) * TOKEN_TILES // 2)
-            nc.scalar.activation(out=sin_table[:, tiles, 0, :], in_=part_turn[:, tiles, :], func=ACT.Sin, scale=2 * math.pi)
+            nc.scalar.activation(out=table[:, tiles, 1, 0, :], in_=part_turn[:, tiles, :], func=ACT.Sin, scale=2 * math.pi)
             nc.scalar.activation(out=part_size[:, tiles, :], in_=part_turn[:, tiles, :], func=ACT.Abs)
-            nc.gpsimd.tensor_scalar(out=sin_table[:, tiles, 1, :], in0=sin_table[:, tiles, 0, :], scalar1=-1.0,
+            nc.scalar.activation(out=table[:, tiles, 0, 0, :], in_=part_size[:, tiles, :], func=ACT.Sin,
+                                 scale=-2 * math.pi, bias=quarter_turn[:])
+            nc.gpsimd.tensor_scalar(out=table[:, tiles, :, 1, :], in0=table[:, tiles, :, 0, :], scalar1=1.0,
                                     scalar2=0.0, op0=ALU.mult, op1=ALU.add)
-        nc.scalar.activation(out=cos_table[:], in_=part_size[:], func=ACT.Sin, scale=-2 * math.pi, bias=quarter_turn[:])
 
-        turn(("x", 0), x_raw[0][:])
-        group_x(0, "vector")
-        for s in range(ROW_TILES):
-            turn((0, s), w_raw[0][:, s, :])
-            group_w(0, s, "vector")
-            if s == 0:
-                quantize_x(0, 1)
-        turn(("x", 1), x_raw[1][:])
-        group_x(1, "vector")
-        quantize_w(0)
+        def turn_x(i, engine, before_projections=False):
+            turn(("x", i), x_raw[i][:], before_projections)
+            group_x(i, engine)
+
+        def turn_w(c, s, engine, before_projections=False):
+            turn((c, s), w_raw[c][:, s, :], before_projections)
+            group_w(c, s, engine)
+
+        def quantize_first_w(h):
+            for g in range(PASSES):
+                quantize_w(0, g * BANK + h * HD, HD)
+
+        new_w_operand(0)
+        turn_x(0, "vector", True)
+        turn_w(0, 0, "vector", True)
+        quantize_x(0, 1)
+        turn_w(0, 1, "vector", True)
+        turn_w(0, 2, "scalar", True)
+        quantize_first_w(0)
+        project(0, [0])
+        mean_square(0, 0)
+        inverse_rms(0, [0])
+        turn_w(0, 3, "vector")
+        turn_x(1, "vector")
+        quantize_first_w(1)
         quantize_x(1, 1)
-        project(0)
-        for i in (2, 3):
-            turn(("x", i), x_raw[i][:])
-            group_x(i, "vector")
+        project(0, [1])
+        turn_x(2, "scalar")
+        products(0, [0])
+        quantize_x(2, 1)
+        mean_square(0, 1)
+        both = list(range(HEADS_PER_BANK))
 
-        for n in range(STEPS + 1):
+        def close(n):
+            c, i = divmod(n, TOKEN_TILES)
+            products(n, both if n > 0 else [1])
+            if c + 1 < CHUNKS and i == (5 if c == 0 else 3):
+                new_w_operand(c + 1)
+                quantize_w(c + 1, 0, PASSES * BANK)
+            if c == 0 and i in (0, 1, 3):
+                quantize_x(*{0: (3, 1), 1: (4, 2), 3: (6, 2)}[i])
+            first, size = group_of[n]
+            if n == STEPS - 1:
+                for lo in range(size):
+                    finish(nc.vector, first, lo, lo + 1)
+            elif n + 1 == first + size:
+                finish(nc.gpsimd, first, 0, size)
+
+        turn_x(3, "scalar")
+        for n in range(1, STEPS):
             c, i = divmod(n, TOKEN_TILES)
             first_turn = 2 if c == 0 else 0
-            if 0 < n < STEPS:
-                project(n)
-            if n < STEPS:
-                mean_square(n, 0)
-            if n > 0:
-                inverse_rms(n - 1)
-            if n < STEPS:
-                mean_square(n, 1)
-            if c == 0 and i < 4:
-                turn(("x", i + 4), x_raw[i + 4][:])
-                group_x(i + 4, "scalar")
-            if c + 1 < CHUNKS:
-                s = i - first_turn
-                if s in (0, 2):
-                    turn((c + 1, s), w_raw[c + 1][:, s, :])
-                    turn((c + 1, s + 1), w_raw[c + 1][:, s + 1, :])
-                if 0 <= s < ROW_TILES:
-                    group_w(c + 1, s, "scalar")
-            if n > 0:
-                products(n - 1)
-            if c + 1 < CHUNKS and i - first_turn == ROW_TILES:
-                quantize_w(c + 1)
-            if c == 0 and i in (0, 2, 4):
-                quantize_x(i + 2, 2)
-            if n > 0:
-                first, size = group_of[n - 1]
-                if n == STEPS:
-                    for lo in range(size):
-                        finish(nc.vector, first, lo, lo + 1)
-                elif n == first + size:
-                    finish(nc.gpsimd, first, 0, size)
-            if i == TOKEN_TILES - 1 and c + 3 < CHUNKS:
+            project(n, both)
+            mean_square(n, 0)
+            inverse_rms(n - 1, both if n > 1 else [1])
+            mean_square(n, 1)
+            if c == 0:
+                for tile in {1: [4, 5], 2: [6], 3: [7]}.get(i, []):
+                    turn_x(tile, "scalar")
+            if c + 1 < CHUNKS and 0 <= i - first_turn < ROW_TILES:
+                turn_w(c + 1, i - first_turn, "scalar")
+            close(n - 1)
+            if i == ROW_TILES + 1 and c + 3 < CHUNKS:
                 load_w(c + 3)
+        inverse_rms(STEPS - 1, both)
+        close(STEPS - 1)

@@ -25,12 +25,14 @@ K_PASS = 512
 PASSES = D // K_PASS
 PASS_WORDS = K_PASS // 2
 BANK = 512
-HEADS_PER_BANK = BANK // HD
 ROW_TILES = BANK // P
 TOKEN_TILES = T // P
 CHUNKS = 2 * E // BANK
-STEPS = CHUNKS * TOKEN_TILES
-GROUP = 4
+UNITS = 8
+ACC_BANKS = 6
+GROUP = 3
+TAIL = 4
+STORE_LAG = 3
 
 
 def tile_mixerdiffattention_pa_kernel(tc, x, Wq, Wk, out_0, out_1):
@@ -39,157 +41,222 @@ def tile_mixerdiffattention_pa_kernel(tc, x, Wq, Wk, out_0, out_1):
     outs = [o.rearrange("b t h d -> (b t) (h d)") for o in (out_0, out_1)]
     chunks_per_weight = E // BANK
 
-    def chunk_rows(c):
-        weight = (Wq, Wk)[c // chunks_per_weight]
-        first = (c % chunks_per_weight) * BANK
-        return weight[first : first + BANK, :]
+    row_units = [[(i, 0), (i, 1)] for i in range(ROW_TILES)]
+    row_units += [[(i, 0), (i + 1, 0)] for i in range(ROW_TILES, TOKEN_TILES, 2)]
+    units = []
+    for c in range(CHUNKS):
+        rows = [("rows", c, vectors) for vectors in row_units]
+        columns = [("columns", c, a) for a in range(2)]
+        units += rows + columns if c + 1 < CHUNKS else [("rows", c, [(i, 0), (i, 1)]) for i in range(TOKEN_TILES)]
+    steps = len(units)
+
+    groups = []
+    for c in range(CHUNKS - 1):
+        groups += [[UNITS * c + GROUP * k + m for m in range(GROUP)] for k in range(2)]
+    groups += [[n, n + 1] for n in range(steps - UNITS, steps, 2)]
+    group_of = {n: group for group in groups for n in group}
 
     with ExitStack() as ctx:
         keep = ctx.enter_context(tc.tile_pool(name="keep", bufs=1))
         w_raw_pool = ctx.enter_context(tc.tile_pool(name="w_raw", bufs=3))
         w_pool = ctx.enter_context(tc.tile_pool(name="w_mx", bufs=2))
-        work = ctx.enter_context(tc.tile_pool(name="work", bufs=3))
-        result_pool = ctx.enter_context(tc.tile_pool(name="result", bufs=4))
+        term_pool = ctx.enter_context(tc.tile_pool(name="terms", bufs=3))
+        column_pool = ctx.enter_context(tc.tile_pool(name="columns", bufs=2))
+        result_pool = ctx.enter_context(tc.tile_pool(name="result", bufs=5))
         small = ctx.enter_context(tc.tile_pool(name="small", bufs=8))
-        turn_psum = ctx.enter_context(tc.psum_pool(name="turn_psum", bufs=2))
-        acc_psum = ctx.enter_context(tc.psum_pool(name="acc_psum", bufs=6))
+        turn_psum = ctx.enter_context(tc.psum_pool(name="turn_psum", bufs=8 - ACC_BANKS))
+        acc_psum = ctx.enter_context(tc.psum_pool(name="acc_psum", bufs=ACC_BANKS))
         ctx.enter_context(tc.manual_schedule())
 
         x_raw = [keep.tile([P, D], BF16, name="x_raw%d" % i) for i in range(TOKEN_TILES)]
-        x_grouped = keep.tile([P, TOKEN_TILES, PASSES * P * 4], BF16, align_bytes=64)
-        x_codes = keep.tile([P, TOKEN_TILES, PASSES * P], U32, align_bytes=64)
-        x_scales = keep.tile([P, TOKEN_TILES, PASSES * P], U8, align_bytes=64)
-        w_raw, w_grouped, w_codes, w_scales = {}, {}, {}, {}
-        turned, acc, mean_sq, inv_rms, terms = {}, {}, {}, {}, {}
+        w_raw, grouped, codes, scales = {}, {}, {}, {}
+        acc, mean_sq, inv_rms, terms, column_terms, column_sums = {}, {}, {}, {}, {}, {}
+        for z in range(2):
+            grouped["x", z] = keep.tile([P, PASSES * BANK * 4], BF16, name="x_grouped%d" % z, align_bytes=64)
+            codes["x", z] = keep.tile([P, PASSES * BANK], U32, name="x_codes%d" % z, align_bytes=64)
+            scales["x", z] = keep.tile([P, PASSES * BANK], U8, name="x_scales%d" % z, align_bytes=64)
 
         def load_x(i):
             nc.sync.dma_start(out=x_raw[i][:], in_=x_rows[i * P : (i + 1) * P, :])
 
         def load_w(c):
             w_raw[c] = w_raw_pool.tile([P, ROW_TILES, D], BF16, name="w_rows")
-            rows = chunk_rows(c).rearrange("(s m) k -> m s k", s=ROW_TILES)
+            first = (c % chunks_per_weight) * BANK
+            rows = (Wq, Wk)[c // chunks_per_weight][first : first + BANK, :].rearrange("(s m) k -> m s k", s=ROW_TILES)
             piece = 1 if c == 0 else ROW_TILES
             for s in range(0, ROW_TILES, piece):
                 nc.sync.dma_start(out=w_raw[c][:, s : s + piece, :], in_=rows[:, s : s + piece, :])
 
-        def turn(key, rows, before_projections=False):
+        def store(c, tiles, column, width, values):
+            first = (c % chunks_per_weight) * BANK + column
+            target = outs[c // chunks_per_weight][tiles[0] * P : (tiles[-1] + 1) * P, first : first + width]
+            nc.sync.dma_start(out=target.rearrange("(i p) n -> p i n", p=P), in_=values.rearrange("p (i n) -> p i n", n=width))
+
+        def turn(rows, operand, s, copy, pool, tag):
             words = rows.bitcast(F32)
-            if before_projections:
-                bank = acc_psum.tile([P, PASSES, 2, P], F32, name="acc")
-            else:
-                bank = turn_psum.tile([P, PASSES, 2, P], F32, name="turned")
+            bank = pool.tile([P, PASSES, 2, P], F32, name=tag)
             for g in range(PASSES):
                 for u in range(2):
                     nc.tensor.transpose(bank[:, g, u, :], words[:, g * PASS_WORDS + u : (g + 1) * PASS_WORDS : 2], identity[:])
-            turned[key] = bank
+            target = grouped[operand][:].bitcast(F32).rearrange("p (g n u) -> p g n u", g=PASSES, u=2)
+            copy(out=target[:, :, s * P : (s + 1) * P, :], in_=bank[:].rearrange("p g u r -> p g r u"))
 
-        def copy_on(engine, out, in_):
-            if engine == "vector":
-                nc.vector.tensor_copy(out=out, in_=in_)
-            else:
-                nc.scalar.copy(out=out, in_=in_)
+        def turn_x(i, copy, pool=turn_psum, tag="turned"):
+            turn(x_raw[i][:], ("x", i // ROW_TILES), i % ROW_TILES, copy, pool, tag)
 
-        def group_x(i, engine):
-            target = x_grouped[:, i, :].bitcast(F32).rearrange("p (g r u) -> p g r u", g=PASSES, u=2)
-            copy_on(engine, target, turned["x", i][:].rearrange("p g u r -> p g r u"))
-
-        def group_w(c, s, engine):
+        def turn_w(c, s, copy, pool=turn_psum, tag="turned"):
             if s == 0:
-                w_grouped[c] = w_pool.tile([P, PASSES * BANK * 4], BF16, name="w_grouped", align_bytes=64)
-            words = w_grouped[c][:].bitcast(F32).rearrange("p (g n u) -> p g n u", g=PASSES, u=2)
-            copy_on(engine, words[:, :, s * P : (s + 1) * P, :], turned[c, s][:].rearrange("p g u r -> p g r u"))
+                grouped["w", c] = w_pool.tile([P, PASSES * BANK * 4], BF16, name="w_grouped", align_bytes=64)
+            turn(w_raw[c][:, s, :], ("w", c), s, copy, pool, tag)
 
-        def quantize_x(first, count):
-            tiles = slice(first, first + count)
+        def quantize(operand, first=0, width=PASSES * BANK):
+            if operand not in codes:
+                codes[operand] = w_pool.tile([P, PASSES * BANK], U32, name="w_codes", align_bytes=64)
+                scales[operand] = w_pool.tile([P, PASSES * BANK], U8, name="w_scales", align_bytes=64)
             nc.vector.quantize_mx(
-                out=x_codes[:, tiles, :].rearrange("p i c -> p (i c)").bitcast(E5M2X4),
-                scales=x_scales[:, tiles, :].rearrange("p i c -> p (i c)"),
-                in_=x_grouped[:, tiles, :].rearrange("p i c -> p (i c)"),
+                out=codes[operand][:, first : first + width].bitcast(E5M2X4),
+                scales=scales[operand][:, first : first + width],
+                in_=grouped[operand][:, 4 * first : 4 * (first + width)],
             )
 
-        def new_w_operand(c):
-            w_codes[c] = w_pool.tile([P, PASSES * BANK], U32, name="w_codes", align_bytes=64)
-            w_scales[c] = w_pool.tile([P, PASSES * BANK], U8, name="w_scales", align_bytes=64)
-
-        def quantize_w(c, first, width):
-            nc.vector.quantize_mx(
-                out=w_codes[c][:, first : first + width].bitcast(E5M2X4),
-                scales=w_scales[c][:, first : first + width],
-                in_=w_grouped[c][:, 4 * first : 4 * (first + width)],
-            )
-
-        def project(n, heads):
-            c, i = divmod(n, TOKEN_TILES)
-            width = len(heads) * HD
-            bank = acc_psum.tile([P, BANK], F32, name="acc")
+        def quantize_rows(operand, first, width):
             for g in range(PASSES):
-                tokens = slice(g * P, (g + 1) * P)
-                features = slice(g * BANK + heads[0] * HD, g * BANK + heads[0] * HD + width)
+                quantize(operand, g * BANK + first, width)
+
+        def multiply(out, stationary, first_m, moving, first_n, width):
+            for g in range(PASSES):
+                m = slice(g * BANK + first_m, g * BANK + first_m + P)
+                n = slice(g * BANK + first_n, g * BANK + first_n + width)
                 nc.tensor.matmul_mx(
-                    out=bank[:, 0:width],
-                    lhsT=x_codes[:, i, tokens].bitcast(E5M2X4),
-                    lhsT_scale=x_scales[:, i, tokens],
-                    rhs=w_codes[c][:, features].bitcast(E5M2X4),
-                    rhs_scale=w_scales[c][:, features],
+                    out=out,
+                    lhsT=codes[stationary][:, m].bitcast(E5M2X4),
+                    lhsT_scale=scales[stationary][:, m],
+                    rhs=codes[moving][:, n].bitcast(E5M2X4),
+                    rhs_scale=scales[moving][:, n],
                     start=(g == 0),
                     stop=(g == PASSES - 1),
                 )
-            for place, h in enumerate(heads):
-                acc[n, h] = bank[:, place * HD : (place + 1) * HD]
 
-        def mean_square(n, h):
-            if h == 0:
-                mean_sq[n] = small.tile([P, HEADS_PER_BANK], F32, name="mean_sq")
+        def project_rows(c, vectors):
+            bank = acc_psum.tile([P, BANK], F32, name="acc")
+            for place, (i, h) in enumerate(vectors):
+                acc[c, i, h] = bank[:, place * HD : (place + 1) * HD]
+            one_tile = len(vectors) == 2 and vectors[0][0] == vectors[1][0]
+            for i, h in vectors[:1] if one_tile else vectors:
+                out, width = (bank[:], BANK) if one_tile else (acc[c, i, h], HD)
+                multiply(out, ("x", i // ROW_TILES), (i % ROW_TILES) * P, ("w", c), h * HD, width)
+
+        def project_columns(c, a):
+            acc[c, a] = acc_psum.tile([P, BANK], F32, name="acc")
+            multiply(acc[c, a][:], ("w", c), HD + a * HALF, ("x", 1), 0, BANK)
+
+        def mean_square(key, place, vector):
+            if place == 0:
+                mean_sq[key] = small.tile([P, 2], F32, name="mean_sq")
             squares = small.tile([P, HD], BF16, name="squares")
-            nc.scalar.activation(
-                out=squares[:], in_=acc[n, h], func=ACT.Square,
-                scale=1.0 / math.sqrt(HD), accum_out=mean_sq[n][:, h : h + 1],
-            )
+            nc.scalar.activation(out=squares[:], in_=vector, func=ACT.Square, scale=1.0 / math.sqrt(HD),
+                                 accum_out=mean_sq[key][:, place : place + 1])
+            release_factors()
 
-        def inverse_rms(n, heads):
-            factors = small.tile([P, len(heads)], F32, name="inv_rms")
-            nc.scalar.activation(out=factors[:], in_=mean_sq[n][:, heads[0] : heads[-1] + 1],
+        def inverse_rms(key, places=(0, 1)):
+            factors = small.tile([P, len(places)], F32, name="inv_rms")
+            nc.scalar.activation(out=factors[:], in_=mean_sq[key][:, places[0] : places[-1] + 1],
                                  func=ACT.Abs_reciprocal_sqrt, bias=eps[:])
-            for place, h in enumerate(heads):
-                inv_rms[n, h] = factors[:, place : place + 1]
+            for m, place in enumerate(places):
+                inv_rms[key, place] = factors[:, m : m + 1]
 
-        def products(n, heads):
-            i = n % TOKEN_TILES
-            first, size = group_of[n]
+        waiting, stores = [], {}
+
+        def release_factors():
+            for key, places in waiting:
+                inverse_rms(key, places)
+            waiting.clear()
+
+        def on_scalar(out, in_):
+            nc.scalar.copy(out=out, in_=in_)
+            release_factors()
+
+        def row_products(n, places=(0, 1)):
+            kind, c, vectors = units[n]
+            first = group_of[n][0]
             if first not in terms:
-                terms[first] = work.tile([P, GROUP * HEADS_PER_BANK, 2, HD], F32, name="terms")
-            for h in heads:
+                terms[first] = term_pool.tile([P, 2 * GROUP, 2, HD], F32, name="terms")
+            for place in places:
+                i, h = vectors[place]
                 nc.vector.scalar_tensor_tensor(
-                    out=terms[first][:, (n - first) * HEADS_PER_BANK + h, :, :],
-                    in0=acc[n, h].unsqueeze(1).to_broadcast([P, 2, HD]),
-                    scalar=inv_rms[n, h],
+                    out=terms[first][:, 2 * (n - first) + place, :, :],
+                    in0=acc[c, i, h].unsqueeze(1).to_broadcast([P, 2, HD]),
+                    scalar=inv_rms[n, place],
                     in1=table[:, i, :, :, :].rearrange("p f a j -> p f (a j)"),
                     op0=ALU.mult, op1=ALU.mult,
                 )
 
-        def finish(engine, first, lo, hi):
-            c, i = divmod(first, TOKEN_TILES)
+        def add_rows(engine, members):
+            first = group_of[members[0]][0]
             result = result_pool.tile([P, GROUP * BANK], F32, name="result")
-            width = (hi - lo) * BANK
-            halves = result[:, 0:width].rearrange("p (v a j) -> p v a j", a=2, j=HALF)
-            vectors = slice(lo * HEADS_PER_BANK, hi * HEADS_PER_BANK)
-            by_cos, by_sin = terms[first][:, vectors, 0, :], terms[first][:, vectors, 1, :]
+            halves = result[:, 0 : len(members) * BANK].rearrange("p (v a j) -> p v a j", a=2, j=HALF)
+            chosen = slice(2 * (members[0] - first), 2 * (members[-1] + 1 - first))
+            by_cos, by_sin = terms[first][:, chosen, 0, :], terms[first][:, chosen, 1, :]
             engine.tensor_tensor(out=halves[:, :, 0, :], in0=by_cos[:, :, 0:HALF], in1=by_sin[:, :, HALF:HD], op=ALU.add)
             engine.tensor_tensor(out=halves[:, :, 1, :], in0=by_cos[:, :, HALF:HD], in1=by_sin[:, :, 0:HALF], op=ALU.subtract)
-            column = (c % chunks_per_weight) * BANK
-            target = outs[c // chunks_per_weight][(i + lo) * P : (i + hi) * P, column : column + BANK]
-            nc.sync.dma_start(
-                out=target.rearrange("(i p) n -> p i n", p=P),
-                in_=result[:, 0:width].rearrange("p (i n) -> p i n", n=BANK),
+            tiles = [i for n in members for i, h in units[n][2] if h == 0]
+            c = units[first][1]
+            both_heads = [i for i in tiles if i < ROW_TILES or c + 1 == CHUNKS]
+            one_head = [i for i in tiles if i not in both_heads]
+            split = len(both_heads) * BANK
+            due = stores.setdefault(members[-1] + STORE_LAG if members[-1] < steps - TAIL else steps, [])
+            if both_heads:
+                due.append((c, both_heads, 0, BANK, result[:, 0:split]))
+            if one_head:
+                due.append((c, one_head, 0, HD, result[:, split : split + len(one_head) * HD]))
+
+        def column_products(c, a):
+            if a == 0:
+                column_terms[c] = column_pool.tile([P, 2, 2, BANK], F32, name="column_terms")
+            nc.vector.tensor_tensor(
+                out=column_terms[c][:, a, :, :],
+                in0=acc[c, a][:].unsqueeze(1).to_broadcast([P, 2, BANK]),
+                in1=turned_table[:, 1 - a : 3 - a, :],
+                op=ALU.mult,
             )
 
-        sizes = [1, 1, 2, 2, 2] + [GROUP] * (2 * CHUNKS - 4) + [2, 2, GROUP]
-        group_of = {}
-        first = 0
-        for size in sizes:
-            for n in range(first, first + size):
-                group_of[n] = (first, size)
-            first += size
+        def add_columns(c):
+            for pair in range(2):
+                bank = turn_psum.tile([P, 2, 2, HALF], F32, name="turned")
+                for place in range(2):
+                    tokens = slice((2 * pair + place) * P, (2 * pair + place + 1) * P)
+                    for half in range(2):
+                        for a in range(2):
+                            nc.tensor.matmul(bank[:, place, half, :], lhsT=column_terms[c][:, a, half, tokens], rhs=identity[:],
+                                             is_transpose=True, start=(a == 0), stop=(a == 1))
+                column_sums[c, pair] = bank[:].rearrange("p v a j -> p v (a j)")
+
+        def scale_columns(c):
+            result = column_pool.tile([P, ROW_TILES, HD], F32, name="column_result")
+
+            def scale(pair, place):
+                nc.scalar.activation(out=result[:, 2 * pair + place, :], in_=column_sums[c, pair][:, place, :],
+                                     func=ACT.Copy, scale=inv_rms[(c, pair), place])
+
+            for pair in range(2):
+                for place in range(2):
+                    mean_square((c, pair), place, column_sums[c, pair][:, place, :])
+                waiting.append(((c, pair), (0, 1)))
+            scale(0, 0)
+            release_factors()
+            scale(0, 1)
+            scale(1, 0)
+            scale(1, 1)
+            store(c, list(range(ROW_TILES, TOKEN_TILES)), HD, HD, result[:].rearrange("p i n -> p (i n)"))
+
+        def turn_table(f):
+            bank = turn_psum.tile([P, ROW_TILES, P], F32, name="turned")
+            for s in range(ROW_TILES):
+                nc.tensor.transpose(bank[:, s, :], table[:, ROW_TILES + s, f, 0, :], identity[:])
+            values = bank[:].rearrange("p s t -> p (s t)")
+            on_scalar(turned_table[:, 1 - f, :], values)
+            if f == 1:
+                nc.scalar.activation(out=turned_table[:, 2, :], in_=values, func=ACT.Copy, scale=-1.0)
 
         load_x(0)
         load_w(0)
@@ -226,84 +293,111 @@ def tile_mixerdiffattention_pa_kernel(tc, x, Wq, Wk, out_0, out_1):
         part_turn = keep.tile([P, TOKEN_TILES, HALF], F32)
         part_size = keep.tile([P, TOKEN_TILES, HALF], F32)
         table = keep.tile([P, TOKEN_TILES, 2, 2, HALF], F32)
-        for i in range(TOKEN_TILES):
-            nc.vector.tensor_scalar(out=whole_turns[:, i, :], in0=rate[:], scalar1=position[:, i : i + 1],
-                                    scalar2=None, op0=ALU.mult)
-        for i in range(TOKEN_TILES):
-            nc.vector.scalar_tensor_tensor(out=part_turn[:, i, :], in0=rate[:], scalar=position[:, i : i + 1],
-                                           in1=whole_turns[:, i, :], op0=ALU.mult, op1=ALU.subtract)
-        for half in range(2):
-            tiles = slice(half * TOKEN_TILES // 2, (half + 1) * TOKEN_TILES // 2)
+        turned_table = keep.tile([P, 3, BANK], F32)
+        for z in range(2):
+            for i in range(z * ROW_TILES, (z + 1) * ROW_TILES):
+                nc.vector.tensor_scalar(out=whole_turns[:, i, :], in0=rate[:], scalar1=position[:, i : i + 1],
+                                        scalar2=None, op0=ALU.mult)
+            for i in range(z * ROW_TILES, (z + 1) * ROW_TILES):
+                nc.vector.scalar_tensor_tensor(out=part_turn[:, i, :], in0=rate[:], scalar=position[:, i : i + 1],
+                                               in1=whole_turns[:, i, :], op0=ALU.mult, op1=ALU.subtract)
+        on_vector = nc.vector.tensor_copy
+        early, late = slice(0, ROW_TILES), slice(ROW_TILES, TOKEN_TILES)
+
+        def sine(tiles):
             nc.scalar.activation(out=table[:, tiles, 1, 0, :], in_=part_turn[:, tiles, :], func=ACT.Sin, scale=2 * math.pi)
-            nc.scalar.activation(out=part_size[:, tiles, :], in_=part_turn[:, tiles, :], func=ACT.Abs)
+
+        def cosine(tiles):
             nc.scalar.activation(out=table[:, tiles, 0, 0, :], in_=part_size[:, tiles, :], func=ACT.Sin,
                                  scale=-2 * math.pi, bias=quarter_turn[:])
-            nc.gpsimd.tensor_scalar(out=table[:, tiles, :, 1, :], in0=table[:, tiles, :, 0, :], scalar1=1.0,
-                                    scalar2=0.0, op0=ALU.mult, op1=ALU.add)
 
-        def turn_x(i, engine, before_projections=False):
-            turn(("x", i), x_raw[i][:], before_projections)
-            group_x(i, engine)
+        sine(early)
+        for tiles in (early, late):
+            nc.scalar.activation(out=part_size[:, tiles, :], in_=part_turn[:, tiles, :], func=ACT.Abs)
+        cosine(early)
+        sine(late)
+        cosine(late)
 
-        def turn_w(c, s, engine, before_projections=False):
-            turn((c, s), w_raw[c][:, s, :], before_projections)
-            group_w(c, s, engine)
+        def repeat_table(z):
+            tiles = slice(z * ROW_TILES, (z + 1) * ROW_TILES)
+            nc.vector.tensor_copy(out=table[:, tiles, :, 1, :], in_=table[:, tiles, :, 0, :])
 
-        def quantize_first_w(h):
-            for g in range(PASSES):
-                quantize_w(0, g * BANK + h * HD, HD)
-
-        new_w_operand(0)
-        turn_x(0, "vector", True)
-        turn_w(0, 0, "vector", True)
-        quantize_x(0, 1)
-        turn_w(0, 1, "vector", True)
-        turn_w(0, 2, "scalar", True)
-        quantize_first_w(0)
-        project(0, [0])
-        mean_square(0, 0)
-        inverse_rms(0, [0])
-        turn_w(0, 3, "vector")
-        turn_x(1, "vector")
-        quantize_first_w(1)
-        quantize_x(1, 1)
-        project(0, [1])
-        turn_x(2, "scalar")
-        products(0, [0])
-        quantize_x(2, 1)
-        mean_square(0, 1)
-        both = list(range(HEADS_PER_BANK))
+        turn_x(0, on_vector, acc_psum, "acc")
+        turn_w(0, 0, on_vector, acc_psum, "acc")
+        quantize_rows(("x", 0), 0, P)
+        turn_w(0, 1, on_vector, acc_psum, "acc")
+        turn_w(0, 2, on_vector, acc_psum, "acc")
+        quantize_rows(("w", 0), 0, HD)
+        turn_w(0, 3, on_vector, acc_psum, "acc")
+        turn_x(1, on_vector, acc_psum, "acc")
+        turn_x(2, on_scalar)
+        project_rows(0, [(0, 0)])
+        mean_square(0, 0, acc[0, 0, 0])
+        inverse_rms(0, (0,))
+        quantize_rows(("w", 0), HD, HD)
+        quantize_rows(("x", 0), P, P)
+        turn_x(3, on_vector)
+        project_rows(0, [(0, 1)])
+        repeat_table(0)
+        mean_square(0, 1, acc[0, 0, 1])
+        waiting.append((0, (1,)))
+        quantize_rows(("x", 0), 2 * P, 2 * P)
+        row_products(0, (0,))
 
         def close(n):
-            c, i = divmod(n, TOKEN_TILES)
-            products(n, both if n > 0 else [1])
-            if c + 1 < CHUNKS and i == (5 if c == 0 else 3):
-                new_w_operand(c + 1)
-                quantize_w(c + 1, 0, PASSES * BANK)
-            if c == 0 and i in (0, 1, 3):
-                quantize_x(*{0: (3, 1), 1: (4, 2), 3: (6, 2)}[i])
-            first, size = group_of[n]
-            if n == STEPS - 1:
-                for lo in range(size):
-                    finish(nc.vector, first, lo, lo + 1)
-            elif n + 1 == first + size:
-                finish(nc.gpsimd, first, 0, size)
+            kind, c, what = units[n]
+            place_in_chunk = n % UNITS
+            if kind == "columns":
+                column_products(c, what)
+                return
+            row_products(n, (0, 1) if n > 0 else (1,))
+            if n in (1, 2):
+                quantize_rows(("x", 1), (n - 1) * HD, HD)
+            if n == 2:
+                repeat_table(1)
+            if c < CHUNKS - 1 and place_in_chunk == (5 if c == 0 else 2):
+                quantize(("w", c + 1))
+            if n == steps - 1:
+                for member in range(steps - TAIL, steps):
+                    add_rows(nc.vector, [member])
+            elif n == group_of[n][-1] and n < steps - TAIL:
+                add_rows(nc.gpsimd, group_of[n])
 
-        turn_x(3, "scalar")
-        for n in range(1, STEPS):
-            c, i = divmod(n, TOKEN_TILES)
-            first_turn = 2 if c == 0 else 0
-            project(n, both)
-            mean_square(n, 0)
-            inverse_rms(n - 1, both if n > 1 else [1])
-            mean_square(n, 1)
-            if c == 0:
-                for tile in {1: [4, 5], 2: [6], 3: [7]}.get(i, []):
-                    turn_x(tile, "scalar")
-            if c + 1 < CHUNKS and 0 <= i - first_turn < ROW_TILES:
-                turn_w(c + 1, i - first_turn, "scalar")
+        add_at = {UNITS * (c + 1) - 1 + ACC_BANKS: c for c in range(CHUNKS - 1)}
+        scale_at = {n + 1: c for n, c in add_at.items()}
+
+        for n in range(1, steps + 1):
+            if n < steps:
+                kind, c, what = units[n]
+                if kind == "rows":
+                    project_rows(c, what)
+                    mean_square(n, 0, acc[(c,) + what[0]])
+                    mean_square(n, 1, acc[(c,) + what[1]])
+                    waiting.append((n, (0, 1)))
+                else:
+                    project_columns(c, what)
+            if n in scale_at:
+                scale_columns(scale_at[n])
+            if n in add_at:
+                add_columns(add_at[n])
+            c, place_in_chunk = divmod(n, UNITS)
+            if n in (1, 2):
+                turn_x(2 * n + 2, on_scalar)
+                turn_x(2 * n + 3, on_scalar)
+            if n in (3, 4):
+                turn_w(1, 2 * n - 6, on_scalar)
+                turn_w(1, 2 * n - 5, on_scalar)
+            if n == 5:
+                turn_table(0)
+                turn_table(1)
+            if 6 <= n < 10:
+                turn_w(2, n - 6, on_scalar)
+            if 1 < c < CHUNKS - 1 and place_in_chunk < ROW_TILES:
+                turn_w(c + 1, place_in_chunk, on_scalar)
+            if waiting and waiting[0][0] == n - 1:
+                release_factors()
             close(n - 1)
-            if i == ROW_TILES + 1 and c + 3 < CHUNKS:
+            for job in stores.get(n, []):
+                store(*job)
+            if place_in_chunk == 5 and c + 3 < CHUNKS:
                 load_w(c + 3)
-        inverse_rms(STEPS - 1, both)
-        close(STEPS - 1)

import math
from contextlib import ExitStack

import concourse.mybir as mybir
from concourse.masks import make_identity

T, D, NH, HD = 1024, 1024, 8, 256
E = NH * HD
HALF = HD // 2
EPS = 2.0 ** -23
ROPE_BASE = 10000.0
FLOPS = 2 * T * D * 2 * E

F32 = mybir.dt.float32
BF16 = mybir.dt.bfloat16
I32 = mybir.dt.int32
U32 = mybir.dt.uint32
U8 = mybir.dt.uint8
E5M2X4 = mybir.dt.float8_e5m2_x4
ALU = mybir.AluOpType
ACT = mybir.ActivationFunctionType

P = 128
K_PASS = 512
PASSES = D // K_PASS
PASS_WORDS = K_PASS // 2
BANK = 512
ROW_TILES = BANK // P
TOKEN_TILES = T // P
CHUNKS = 2 * E // BANK
UNITS = 8
ACC_BANKS = 6
GROUP = 3
TAIL = 4
STORE_LAG = 3


def tile_mixerdiffattention_pa_kernel(tc, x, Wq, Wk, out_0, out_1):
    nc = tc.nc
    x_rows = x.rearrange("b t d -> (b t) d")
    outs = [o.rearrange("b t h d -> (b t) (h d)") for o in (out_0, out_1)]
    chunks_per_weight = E // BANK

    row_units = [[(i, 0), (i, 1)] for i in range(ROW_TILES)]
    row_units += [[(i, 0), (i + 1, 0)] for i in range(ROW_TILES, TOKEN_TILES, 2)]
    units = []
    for c in range(CHUNKS):
        rows = [("rows", c, vectors) for vectors in row_units]
        columns = [("columns", c, a) for a in range(2)]
        units += rows + columns if c + 1 < CHUNKS else [("rows", c, [(i, 0), (i, 1)]) for i in range(TOKEN_TILES)]
    steps = len(units)

    groups = []
    for c in range(CHUNKS - 1):
        groups += [[UNITS * c + GROUP * k + m for m in range(GROUP)] for k in range(2)]
    groups += [[n, n + 1] for n in range(steps - UNITS, steps, 2)]
    group_of = {n: group for group in groups for n in group}

    with ExitStack() as ctx:
        keep = ctx.enter_context(tc.tile_pool(name="keep", bufs=1))
        w_raw_pool = ctx.enter_context(tc.tile_pool(name="w_raw", bufs=3))
        w_pool = ctx.enter_context(tc.tile_pool(name="w_mx", bufs=2))
        term_pool = ctx.enter_context(tc.tile_pool(name="terms", bufs=3))
        column_pool = ctx.enter_context(tc.tile_pool(name="columns", bufs=2))
        result_pool = ctx.enter_context(tc.tile_pool(name="result", bufs=5))
        small = ctx.enter_context(tc.tile_pool(name="small", bufs=8))
        turn_psum = ctx.enter_context(tc.psum_pool(name="turn_psum", bufs=8 - ACC_BANKS))
        acc_psum = ctx.enter_context(tc.psum_pool(name="acc_psum", bufs=ACC_BANKS))
        ctx.enter_context(tc.manual_schedule())

        x_raw = [keep.tile([P, D], BF16, name="x_raw%d" % i) for i in range(TOKEN_TILES)]
        w_raw, grouped, codes, scales = {}, {}, {}, {}
        acc, mean_sq, inv_rms, terms, column_terms, column_sums = {}, {}, {}, {}, {}, {}
        for z in range(2):
            grouped["x", z] = keep.tile([P, PASSES * BANK * 4], BF16, name="x_grouped%d" % z, align_bytes=64)
            codes["x", z] = keep.tile([P, PASSES * BANK], U32, name="x_codes%d" % z, align_bytes=64)
            scales["x", z] = keep.tile([P, PASSES * BANK], U8, name="x_scales%d" % z, align_bytes=64)

        def load_x(i):
            nc.sync.dma_start(out=x_raw[i][:], in_=x_rows[i * P : (i + 1) * P, :])

        def load_w(c):
            w_raw[c] = w_raw_pool.tile([P, ROW_TILES, D], BF16, name="w_rows")
            first = (c % chunks_per_weight) * BANK
            rows = (Wq, Wk)[c // chunks_per_weight][first : first + BANK, :].rearrange("(s m) k -> m s k", s=ROW_TILES)
            piece = 1 if c == 0 else ROW_TILES
            for s in range(0, ROW_TILES, piece):
                nc.sync.dma_start(out=w_raw[c][:, s : s + piece, :], in_=rows[:, s : s + piece, :])

        def store(c, tiles, column, width, values):
            first = (c % chunks_per_weight) * BANK + column
            target = outs[c // chunks_per_weight][tiles[0] * P : (tiles[-1] + 1) * P, first : first + width]
            nc.sync.dma_start(out=target.rearrange("(i p) n -> p i n", p=P), in_=values.rearrange("p (i n) -> p i n", n=width))

        def turn(rows, operand, s, copy, pool, tag):
            words = rows.bitcast(F32)
            bank = pool.tile([P, PASSES, 2, P], F32, name=tag)
            for g in range(PASSES):
                for u in range(2):
                    nc.tensor.transpose(bank[:, g, u, :], words[:, g * PASS_WORDS + u : (g + 1) * PASS_WORDS : 2], identity[:])
            target = grouped[operand][:].bitcast(F32).rearrange("p (g n u) -> p g n u", g=PASSES, u=2)
            copy(out=target[:, :, s * P : (s + 1) * P, :], in_=bank[:].rearrange("p g u r -> p g r u"))

        def turn_x(i, copy, pool=turn_psum, tag="turned"):
            turn(x_raw[i][:], ("x", i // ROW_TILES), i % ROW_TILES, copy, pool, tag)

        def turn_w(c, s, copy, pool=turn_psum, tag="turned"):
            if s == 0:
                grouped["w", c] = w_pool.tile([P, PASSES * BANK * 4], BF16, name="w_grouped", align_bytes=64)
            turn(w_raw[c][:, s, :], ("w", c), s, copy, pool, tag)

        def quantize(operand, first=0, width=PASSES * BANK):
            if operand not in codes:
                codes[operand] = w_pool.tile([P, PASSES * BANK], U32, name="w_codes", align_bytes=64)
                scales[operand] = w_pool.tile([P, PASSES * BANK], U8, name="w_scales", align_bytes=64)
            nc.vector.quantize_mx(
                out=codes[operand][:, first : first + width].bitcast(E5M2X4),
                scales=scales[operand][:, first : first + width],
                in_=grouped[operand][:, 4 * first : 4 * (first + width)],
            )

        def quantize_rows(operand, first, width):
            for g in range(PASSES):
                quantize(operand, g * BANK + first, width)

        def multiply(out, stationary, first_m, moving, first_n, width):
            for g in range(PASSES):
                m = slice(g * BANK + first_m, g * BANK + first_m + P)
                n = slice(g * BANK + first_n, g * BANK + first_n + width)
                nc.tensor.matmul_mx(
                    out=out,
                    lhsT=codes[stationary][:, m].bitcast(E5M2X4),
                    lhsT_scale=scales[stationary][:, m],
                    rhs=codes[moving][:, n].bitcast(E5M2X4),
                    rhs_scale=scales[moving][:, n],
                    start=(g == 0),
                    stop=(g == PASSES - 1),
                )

        def project_rows(c, vectors):
            bank = acc_psum.tile([P, BANK], F32, name="acc")
            for place, (i, h) in enumerate(vectors):
                acc[c, i, h] = bank[:, place * HD : (place + 1) * HD]
            one_tile = len(vectors) == 2 and vectors[0][0] == vectors[1][0]
            for i, h in vectors[:1] if one_tile else vectors:
                out, width = (bank[:], BANK) if one_tile else (acc[c, i, h], HD)
                multiply(out, ("x", i // ROW_TILES), (i % ROW_TILES) * P, ("w", c), h * HD, width)

        def project_columns(c, a):
            acc[c, a] = acc_psum.tile([P, BANK], F32, name="acc")
            multiply(acc[c, a][:], ("w", c), HD + a * HALF, ("x", 1), 0, BANK)

        def mean_square(key, place, vector):
            if place == 0:
                mean_sq[key] = small.tile([P, 2], F32, name="mean_sq")
            squares = small.tile([P, HD], BF16, name="squares")
            nc.scalar.activation(out=squares[:], in_=vector, func=ACT.Square, scale=1.0 / math.sqrt(HD),
                                 accum_out=mean_sq[key][:, place : place + 1])
            release_factors()

        def inverse_rms(key, places=(0, 1)):
            factors = small.tile([P, len(places)], F32, name="inv_rms")
            nc.scalar.activation(out=factors[:], in_=mean_sq[key][:, places[0] : places[-1] + 1],
                                 func=ACT.Abs_reciprocal_sqrt, bias=eps[:])
            for m, place in enumerate(places):
                inv_rms[key, place] = factors[:, m : m + 1]

        waiting, stores = [], {}

        def release_factors():
            for key, places in waiting:
                inverse_rms(key, places)
            waiting.clear()

        def on_scalar(out, in_):
            nc.scalar.copy(out=out, in_=in_)
            release_factors()

        def row_products(n, places=(0, 1)):
            kind, c, vectors = units[n]
            first = group_of[n][0]
            if first not in terms:
                terms[first] = term_pool.tile([P, 2 * GROUP, 2, HD], F32, name="terms")
            for place in places:
                i, h = vectors[place]
                nc.vector.scalar_tensor_tensor(
                    out=terms[first][:, 2 * (n - first) + place, :, :],
                    in0=acc[c, i, h].unsqueeze(1).to_broadcast([P, 2, HD]),
                    scalar=inv_rms[n, place],
                    in1=table[:, i, :, :, :].rearrange("p f a j -> p f (a j)"),
                    op0=ALU.mult, op1=ALU.mult,
                )

        def add_rows(engine, members):
            first = group_of[members[0]][0]
            result = result_pool.tile([P, GROUP * BANK], F32, name="result")
            halves = result[:, 0 : len(members) * BANK].rearrange("p (v a j) -> p v a j", a=2, j=HALF)
            chosen = slice(2 * (members[0] - first), 2 * (members[-1] + 1 - first))
            by_cos, by_sin = terms[first][:, chosen, 0, :], terms[first][:, chosen, 1, :]
            engine.tensor_tensor(out=halves[:, :, 0, :], in0=by_cos[:, :, 0:HALF], in1=by_sin[:, :, HALF:HD], op=ALU.add)
            engine.tensor_tensor(out=halves[:, :, 1, :], in0=by_cos[:, :, HALF:HD], in1=by_sin[:, :, 0:HALF], op=ALU.subtract)
            tiles = [i for n in members for i, h in units[n][2] if h == 0]
            c = units[first][1]
            both_heads = [i for i in tiles if i < ROW_TILES or c + 1 == CHUNKS]
            one_head = [i for i in tiles if i not in both_heads]
            split = len(both_heads) * BANK
            due = stores.setdefault(members[-1] + STORE_LAG if members[-1] < steps - TAIL else steps, [])
            if both_heads:
                due.append((c, both_heads, 0, BANK, result[:, 0:split]))
            if one_head:
                due.append((c, one_head, 0, HD, result[:, split : split + len(one_head) * HD]))

        def column_products(c, a):
            if a == 0:
                column_terms[c] = column_pool.tile([P, 2, 2, BANK], F32, name="column_terms")
            nc.vector.tensor_tensor(
                out=column_terms[c][:, a, :, :],
                in0=acc[c, a][:].unsqueeze(1).to_broadcast([P, 2, BANK]),
                in1=turned_table[:, 1 - a : 3 - a, :],
                op=ALU.mult,
            )

        def add_columns(c):
            for pair in range(2):
                bank = turn_psum.tile([P, 2, 2, HALF], F32, name="turned")
                for place in range(2):
                    tokens = slice((2 * pair + place) * P, (2 * pair + place + 1) * P)
                    for half in range(2):
                        for a in range(2):
                            nc.tensor.matmul(bank[:, place, half, :], lhsT=column_terms[c][:, a, half, tokens], rhs=identity[:],
                                             is_transpose=True, start=(a == 0), stop=(a == 1))
                column_sums[c, pair] = bank[:].rearrange("p v a j -> p v (a j)")

        def scale_columns(c):
            result = column_pool.tile([P, ROW_TILES, HD], F32, name="column_result")

            def scale(pair, place):
                nc.scalar.activation(out=result[:, 2 * pair + place, :], in_=column_sums[c, pair][:, place, :],
                                     func=ACT.Copy, scale=inv_rms[(c, pair), place])

            for pair in range(2):
                for place in range(2):
                    mean_square((c, pair), place, column_sums[c, pair][:, place, :])
                waiting.append(((c, pair), (0, 1)))
            scale(0, 0)
            release_factors()
            scale(0, 1)
            scale(1, 0)
            scale(1, 1)
            store(c, list(range(ROW_TILES, TOKEN_TILES)), HD, HD, result[:].rearrange("p i n -> p (i n)"))

        def turn_table(f):
            bank = turn_psum.tile([P, ROW_TILES, P], F32, name="turned")
            for s in range(ROW_TILES):
                nc.tensor.transpose(bank[:, s, :], table[:, ROW_TILES + s, f, 0, :], identity[:])
            values = bank[:].rearrange("p s t -> p (s t)")
            on_scalar(turned_table[:, 1 - f, :], values)
            if f == 1:
                nc.scalar.activation(out=turned_table[:, 2, :], in_=values, func=ACT.Copy, scale=-1.0)

        load_x(0)
        load_w(0)
        for i in range(1, TOKEN_TILES):
            load_x(i)
        load_w(1)
        load_w(2)

        identity = keep.tile([P, P], F32)
        make_identity(nc, identity[:])
        position = keep.tile([P, TOKEN_TILES], F32)
        nc.gpsimd.iota(position[:], pattern=[[P, TOKEN_TILES]], base=0, channel_multiplier=1,
                       allow_small_or_imprecise_dtypes=True)

        ones = keep.tile([P, 1], F32)
        nc.vector.memset(ones[:], 1.0)
        eps = keep.tile([P, 1], F32)
        nc.vector.memset(eps[:], EPS)
        quarter_turn = keep.tile([P, 1], F32)
        nc.vector.tensor_scalar(out=quarter_turn[:], in0=ones[:], scalar1=math.pi / 2, scalar2=None, op0=ALU.mult)
        ratio = ROPE_BASE ** (-1.0 / HALF)
        rate = keep.tile([P, HALF], F32)
        known = 4
        for j in range(known):
            nc.vector.tensor_scalar(out=rate[:, j : j + 1], in0=ones[:], scalar1=ratio ** j / (2 * math.pi),
                                    scalar2=None, op0=ALU.mult)
        for radix in (4, 8):
            for m in range(1, radix):
                nc.vector.tensor_scalar(out=rate[:, m * known : (m + 1) * known], in0=rate[:, 0:known],
                                        scalar1=ratio ** (m * known), scalar2=None, op0=ALU.mult)
            known = known * radix

        whole_turns = keep.tile([P, TOKEN_TILES, HALF], I32)
        part_turn = keep.tile([P, TOKEN_TILES, HALF], F32)
        part_size = keep.tile([P, TOKEN_TILES, HALF], F32)
        table = keep.tile([P, TOKEN_TILES, 2, 2, HALF], F32)
        turned_table = keep.tile([P, 3, BANK], F32)
        for z in range(2):
            for i in range(z * ROW_TILES, (z + 1) * ROW_TILES):
                nc.vector.tensor_scalar(out=whole_turns[:, i, :], in0=rate[:], scalar1=position[:, i : i + 1],
                                        scalar2=None, op0=ALU.mult)
            for i in range(z * ROW_TILES, (z + 1) * ROW_TILES):
                nc.vector.scalar_tensor_tensor(out=part_turn[:, i, :], in0=rate[:], scalar=position[:, i : i + 1],
                                               in1=whole_turns[:, i, :], op0=ALU.mult, op1=ALU.subtract)
        on_vector = nc.vector.tensor_copy
        early, late = slice(0, ROW_TILES), slice(ROW_TILES, TOKEN_TILES)

        def sine(tiles):
            nc.scalar.activation(out=table[:, tiles, 1, 0, :], in_=part_turn[:, tiles, :], func=ACT.Sin, scale=2 * math.pi)

        def cosine(tiles):
            nc.scalar.activation(out=table[:, tiles, 0, 0, :], in_=part_size[:, tiles, :], func=ACT.Sin,
                                 scale=-2 * math.pi, bias=quarter_turn[:])

        sine(early)
        for tiles in (early, late):
            nc.scalar.activation(out=part_size[:, tiles, :], in_=part_turn[:, tiles, :], func=ACT.Abs)
        cosine(early)
        sine(late)
        cosine(late)

        def repeat_table(z):
            tiles = slice(z * ROW_TILES, (z + 1) * ROW_TILES)
            nc.vector.tensor_copy(out=table[:, tiles, :, 1, :], in_=table[:, tiles, :, 0, :])

        turn_x(0, on_vector, acc_psum, "acc")
        turn_w(0, 0, on_vector, acc_psum, "acc")
        quantize_rows(("x", 0), 0, P)
        turn_w(0, 1, on_vector, acc_psum, "acc")
        turn_w(0, 2, on_vector, acc_psum, "acc")
        quantize_rows(("w", 0), 0, HD)
        turn_w(0, 3, on_vector, acc_psum, "acc")
        turn_x(1, on_vector, acc_psum, "acc")
        turn_x(2, on_scalar)
        project_rows(0, [(0, 0)])
        mean_square(0, 0, acc[0, 0, 0])
        inverse_rms(0, (0,))
        quantize_rows(("w", 0), HD, HD)
        quantize_rows(("x", 0), P, P)
        turn_x(3, on_vector)
        project_rows(0, [(0, 1)])
        repeat_table(0)
        mean_square(0, 1, acc[0, 0, 1])
        waiting.append((0, (1,)))
        quantize_rows(("x", 0), 2 * P, 2 * P)
        row_products(0, (0,))

        def close(n):
            kind, c, what = units[n]
            place_in_chunk = n % UNITS
            if kind == "columns":
                column_products(c, what)
                return
            row_products(n, (0, 1) if n > 0 else (1,))
            if n in (1, 2):
                quantize_rows(("x", 1), (n - 1) * HD, HD)
            if n == 2:
                repeat_table(1)
            if c < CHUNKS - 1 and place_in_chunk == (5 if c == 0 else 2):
                quantize(("w", c + 1))
            if n == steps - 1:
                for member in range(steps - TAIL, steps):
                    add_rows(nc.vector, [member])
            elif n == group_of[n][-1] and n < steps - TAIL:
                add_rows(nc.gpsimd, group_of[n])

        add_at = {UNITS * (c + 1) - 1 + ACC_BANKS: c for c in range(CHUNKS - 1)}
        scale_at = {n + 1: c for n, c in add_at.items()}

        for n in range(1, steps + 1):
            if n < steps:
                kind, c, what = units[n]
                if kind == "rows":
                    project_rows(c, what)
                    mean_square(n, 0, acc[(c,) + what[0]])
                    mean_square(n, 1, acc[(c,) + what[1]])
                    waiting.append((n, (0, 1)))
                else:
                    project_columns(c, what)
            if n in scale_at:
                scale_columns(scale_at[n])
            if n in add_at:
                add_columns(add_at[n])
            c, place_in_chunk = divmod(n, UNITS)
            if n in (1, 2):
                turn_x(2 * n + 2, on_scalar)
                turn_x(2 * n + 3, on_scalar)
            if n in (3, 4):
                turn_w(1, 2 * n - 6, on_scalar)
                turn_w(1, 2 * n - 5, on_scalar)
            if n == 5:
                turn_table(0)
                turn_table(1)
            if 6 <= n < 10:
                turn_w(2, n - 6, on_scalar)
            if 1 < c < CHUNKS - 1 and place_in_chunk < ROW_TILES:
                turn_w(c + 1, place_in_chunk, on_scalar)
            if waiting and waiting[0][0] == n - 1:
                release_factors()
            close(n - 1)
            for job in stores.get(n, []):
                store(*job)
            if place_in_chunk == 5 and c + 3 < CHUNKS:
                load_w(c + 3)
